import numpy as np
import ml_dtypes


def mxq(x, axis, fmt="e4m3"):
    dtype, down = {"e4m3": (ml_dtypes.float8_e4m3fn, 7), "e5m2": (ml_dtypes.float8_e5m2, 14)}[fmt]
    v = np.moveaxis(np.asarray(x, np.float32).astype(ml_dtypes.bfloat16).astype(np.float64), axis, -1)
    blocks = v.reshape(v.shape[:-1] + (-1, 32))
    amax = np.abs(blocks).max(-1, keepdims=True)
    byte = np.maximum(np.where(amax > 0, np.frexp(amax)[1] - 1 + 127, 0) - down, 1)
    scale = np.exp2(byte - 127.0)
    codes = (blocks / scale).astype(np.float32).astype(dtype).astype(np.float64)
    return np.moveaxis((codes * scale).reshape(v.shape), -1, axis)


WIDE = False


def mx_kscale(k):
    if not WIDE:
        return np.ones(k)
    levels = np.array([20, -20, 10, -10, 0])
    a = np.random.permutation(np.resize(levels, k // 512 * 4)).reshape(k // 512, 4)
    idx = np.arange(k)
    return np.exp2(a[idx // 512, idx % 128 // 32])


BF16 = ml_dtypes.bfloat16


def bf(x):
    return np.asarray(x, np.float32).astype(BF16)


def f64(x):
    return np.asarray(x).astype(np.float64)


DEGREE = 5
A = 1.0
B = 1.0
IN_F = 1024
OUT_F = 1024
BATCH = 512


def silu(v):
    return v / (1.0 + np.exp(-v))


def dsilu(v):
    sg = 1.0 / (1.0 + np.exp(-v))
    return sg * (1.0 + v * (1.0 - sg))


def _coefs(k):
    alpha_n = 2.0 * k * (k + A + B) * (2 * k + A + B - 2)
    beta_n = (2 * k + A + B - 1) * (A ** 2 - B ** 2)
    gamma_n = (2 * k + A + B - 2) * (2 * k + A + B - 1) * (2 * k + A + B)
    delta_n = 2.0 * (k + A - 1) * (k + B - 1) * (2 * k + A + B)
    return alpha_n, beta_n, gamma_n, delta_n


def _jacobi_polynomials(x):
    t = np.tanh(x)
    polys = [np.ones_like(t)]
    if DEGREE >= 1:
        polys.append(0.5 * (2.0 * (A + 1.0) * t + (A - B)))
    for k in range(2, DEGREE + 1):
        alpha_n, beta_n, gamma_n, delta_n = _coefs(k)
        Acoef = (beta_n + alpha_n * t) / gamma_n
        Bcoef = delta_n / gamma_n
        polys.append(Acoef * polys[k - 1] - Bcoef * polys[k - 2])
    return np.stack(polys, axis=-1)


def _jacobi_derivatives(x):
    t = np.tanh(x)
    polys = [np.ones_like(t), 0.5 * (2.0 * (A + 1.0) * t + (A - B))]
    q = [np.zeros_like(t), (A + 1.0) * np.ones_like(t)]
    for k in range(2, DEGREE + 1):
        alpha_n, beta_n, gamma_n, delta_n = _coefs(k)
        Acoef = (beta_n + alpha_n * t) / gamma_n
        Bcoef = delta_n / gamma_n
        polys.append(Acoef * polys[k - 1] - Bcoef * polys[k - 2])
        q.append((alpha_n / gamma_n) * polys[k - 1] + Acoef * q[k - 1] - Bcoef * q[k - 2])
    return np.stack(q[1:], axis=1) * (1.0 - t * t)[:, None, :]


def setup_inputs():
    u = mx_kscale(OUT_F)
    x = np.random.standard_normal((BATCH, IN_F))
    base_weight = np.random.standard_normal((OUT_F, IN_F)) * 0.04 / u[:, None]
    jacobi_coeffs = np.random.standard_normal((OUT_F, IN_F, DEGREE + 1)) * 0.02 / u[:, None, None]
    bias = np.random.standard_normal(OUT_F) * 0.3
    g = np.random.standard_normal((BATCH, OUT_F)) * np.exp2(np.random.randint(-12, 1, (BATCH, 1))) * u
    return {"x": bf(x), "base_weight": bf(base_weight), "jacobi_coeffs": bf(jacobi_coeffs),
            "bias": bf(bias), "grad_out": bf(g)}


def reference(x, base_weight, jacobi_coeffs, bias, grad_out):
    x = f64(x)
    gq = mxq(f64(grad_out), 1, "e5m2")
    hb = gq @ mxq(f64(base_weight), 0, "e4m3")
    Cf = f64(jacobi_coeffs)[:, :, 1:].transpose(0, 2, 1).reshape(OUT_F, DEGREE * IN_F)
    hj = (gq @ mxq(Cf, 0, "e4m3")).reshape(x.shape[0], DEGREE, IN_F)
    return dsilu(x) * hb + (_jacobi_derivatives(x) * hj).sum(axis=1)

@@ -1,0 +1,339 @@
+from contextlib import ExitStack
+import math
+
+import concourse.mybir as mybir
+from concourse.masks import make_identity
+
+F32 = mybir.dt.float32
+BF16 = mybir.dt.bfloat16
+U32 = mybir.dt.uint32
+U8 = mybir.dt.uint8
+E4M3X4 = mybir.dt.float8_e4m3fn_x4
+E5M2X4 = mybir.dt.float8_e5m2_x4
+ACT = mybir.ActivationFunctionType
+ALU = mybir.AluOpType
+
+P = 128
+BATCH = 512
+IN_F = 1024
+OUT_F = 1024
+DEGREE = 5
+NB = BATCH // P
+NG = OUT_F // 512
+BLK = 256
+NBLK = IN_F // BLK
+TILE_I = 128
+
+FLOPS = 2 * (DEGREE + 1) * BATCH * IN_F * OUT_F
+BYTES = 2 * (2 * BATCH * IN_F + IN_F * OUT_F * (DEGREE + 1)) + 4 * BATCH * IN_F
+
+PIN = True
+V_TILES = (0,)
+W_ON_V = (0, 1, 2, 3)
+LEAD_R = 3
+LEAD_Q = 2
+LEAD_M = 1
+LAST_ON_V = False
+
+
+def derivative_polynomials():
+    polys = [[1.0], [0.0, 2.0]]
+    for k in range(2, DEGREE + 1):
+        a_k = k * (k + 2.0) / ((2.0 * k + 1.0) * (k + 1.0))
+        b_k = k / (2.0 * k + 1.0)
+        nxt = [0.0] + [a_k * c for c in polys[k - 1]]
+        for n, c in enumerate(polys[k - 2]):
+            nxt[n] -= b_k * c
+        polys.append(nxt)
+    return [[n * c for n, c in enumerate(p)][1:] for p in polys]
+
+
+def tile_jacobikanlinear_kernel(tc, x, base_weight, jacobi_coeffs, bias, grad_out, out):
+    nc = tc.nc
+    q = derivative_polynomials()
+    c2 = q[2][1]
+    c30, c31 = q[3][0], q[3][2]
+    c40, c41 = q[4][1], q[4][3]
+    c50, c51, c52 = q[5][0], q[5][2], q[5][4]
+    lam = math.sqrt(c31)
+    r3 = c30 / c31
+    r4 = c40 / c41
+    alpha = c51 / (2.0 * c52)
+    beta = c50 / c52 - alpha * alpha
+    ks = lam * c52 / c31
+
+    x_v = x.rearrange("(n p) i -> p n i", p=P)
+    g_v = grad_out.rearrange("(n p) o -> p n o", p=P)
+    out_v = out.rearrange("(n p) i -> p n i", p=P)
+
+    def copy_on(on_vector, dst, src):
+        if on_vector:
+            nc.vector.tensor_copy(out=dst, in_=src)
+        else:
+            nc.scalar.copy(out=dst, in_=src)
+
+    with ExitStack() as ctx:
+        if PIN:
+            ctx.enter_context(tc.manual_schedule())
+        keep = ctx.enter_context(tc.tile_pool(name="keep", bufs=1))
+        ring = ctx.enter_context(tc.tile_pool(name="ring", bufs=4))
+        wring = ctx.enter_context(tc.tile_pool(name="wring", bufs=4))
+        stage = ctx.enter_context(tc.tile_pool(name="stage", bufs=4))
+        codes_a = ctx.enter_context(tc.tile_pool(name="codes_a", bufs=6))
+        codes_b = ctx.enter_context(tc.tile_pool(name="codes_b", bufs=4))
+        sig = ctx.enter_context(tc.tile_pool(name="sig", bufs=2))
+        fac = ctx.enter_context(tc.tile_pool(name="fac", bufs=3))
+        work = ctx.enter_context(tc.tile_pool(name="work", bufs=2))
+        work2 = ctx.enter_context(tc.tile_pool(name="work2", bufs=3))
+        psum = ctx.enter_context(tc.psum_pool(name="psum", bufs=8))
+
+        ident = keep.tile([P, P], F32, name="ident")
+        make_identity(nc, ident[:])
+
+        x_sb = keep.tile([P, NB, IN_F], BF16, name="x_sb")
+        nc.sync.dma_start(out=x_sb[:], in_=x_v)
+        g_sb = ring.tile([P, NB, OUT_F], BF16, tag="stream", name="g_sb", align_bytes=64)
+        nc.sync.dma_start(out=g_sb[:], in_=g_v)
+        g_grp = ring.tile([P, 2 * NB * P * 4], BF16, tag="stream", name="g_grp", align_bytes=64)
+
+        c_raw = {}
+        w_raw = {}
+
+        def load_block(blk):
+            for g in range(NG):
+                raw = ring.tile([P, 4, BLK * 6], BF16, tag="stream", name="c_raw", align_bytes=64)
+                nc.sync.dma_start(
+                    out=raw[:],
+                    in_=jacobi_coeffs[512 * g : 512 * (g + 1), BLK * blk : BLK * (blk + 1), :].rearrange(
+                        "(p j) i k -> p j (i k)", j=4
+                    ),
+                )
+                c_raw[(blk, g)] = raw
+            for g in range(NG):
+                raw = wring.tile([P, 4, BLK], BF16, tag="w_raw", name="w_raw")
+                nc.sync.dma_start(
+                    out=raw[:],
+                    in_=base_weight[512 * g : 512 * (g + 1), BLK * blk : BLK * (blk + 1)].rearrange(
+                        "(p j) c -> p j c", j=4
+                    ),
+                )
+                w_raw[(blk, g)] = raw
+
+        load_block(0)
+
+        nf0 = {}
+
+        def silu_grad(blks):
+            s_t = {}
+            for blk in blks:
+                cs = slice(BLK * blk, BLK * (blk + 1))
+                s_t[blk] = sig.tile([P, NB, BLK], F32, tag="s", name="s_sb")
+                nc.scalar.activation(out=s_t[blk][:], in_=x_sb[:, :, cs], func=ACT.Sigmoid)
+            return s_t
+
+        def silu_grad_v(blks, s_t):
+            for blk in blks:
+                cs = slice(BLK * blk, BLK * (blk + 1))
+                nf0[blk] = keep.tile([P, NB, BLK], F32, name="nf0_%d" % blk)
+                nc.vector.scalar_tensor_tensor(
+                    out=nf0[blk][:], in0=s_t[blk][:], scalar=-1.0, in1=x_sb[:, :, cs], op0=ALU.add, op1=ALU.mult
+                )
+            for blk in blks:
+                nc.vector.scalar_tensor_tensor(
+                    out=nf0[blk][:], in0=nf0[blk][:], scalar=-1.0, in1=s_t[blk][:], op0=ALU.add, op1=ALU.mult
+                )
+
+        s_first = silu_grad((0, 1))
+        silu_grad_v((0, 1), s_first)
+        s_second = silu_grad((2, 3))
+
+        g32 = g_sb[:].bitcast(F32).rearrange("p n (g w u) -> p n g w u", g=NG, u=2)
+        g_grp32 = g_grp[:].bitcast(F32).rearrange("p (s b u) -> p s b u", s=NG * NB, u=2)
+        for pr in range(NG * NB // 2):
+            gt = psum.tile([P, 2, 2, P], F32, tag="bank", name="gt")
+            for h in range(2):
+                g, bt = divmod(2 * pr + h, NB)
+                for u in range(2):
+                    nc.tensor.transpose(gt[:, h, u, :], g32[:, bt, g, :, u], ident[:])
+            nc.vector.tensor_copy(
+                out=g_grp32[:, 2 * pr : 2 * pr + 2, :, :], in_=gt[:].rearrange("p h u b -> p h b u")
+            )
+        g_codes = keep.tile([P, NG * NB * P], U32, name="g_codes", align_bytes=64)
+        g_scales = keep.tile([P, NG * NB * P], U8, name="g_scales", align_bytes=64)
+        nc.vector.quantize_mx(out=g_codes[:].bitcast(E5M2X4), scales=g_scales[:], in_=g_grp[:])
+
+        units = []
+        for blk in range(NBLK):
+            units.extend([("A", 2 * blk), ("B", blk), ("A", 2 * blk + 1)])
+        n_units = len(units)
+
+        grouped = {}
+        opnd = {}
+        banks = {}
+        facs = {}
+        res = {}
+
+        def activations(blk):
+            cs = slice(BLK * blk, BLK * (blk + 1))
+            th = fac.tile([P, NB, BLK], F32, tag="th", name="th")
+            nc.scalar.activation(out=th[:], in_=x_sb[:, :, cs], func=ACT.Tanh)
+            ut = fac.tile([P, NB, BLK], F32, tag="ut", name="ut")
+            nc.scalar.activation(out=ut[:], in_=th[:], func=ACT.Square, scale=math.sqrt(lam))
+            sq = fac.tile([P, NB, BLK], F32, tag="sq", name="sq")
+            nc.scalar.activation(
+                out=sq[:], in_=ut[:], func=ACT.Square, scale=math.sqrt(ks) / lam, bias=math.sqrt(ks) * alpha
+            )
+            facs[blk] = (th, ut, sq)
+
+        def regroup(unit):
+            kind, n = unit
+            tiles = []
+            for g in range(NG):
+                if kind == "A":
+                    blk, h = divmod(n, 2)
+                    view = c_raw[(blk, g)][:].rearrange("p j (i k) -> p i j k", k=6)
+                    ga = stage.tile([P, TILE_I, 4, 4], BF16, tag="grpa", name="ga", align_bytes=64)
+                    copy_on(
+                        n in V_TILES,
+                        ga[:].rearrange("p i k j -> p i j k"),
+                        view[:, TILE_I * h : TILE_I * (h + 1), :, 1:5],
+                    )
+                    tiles.append(ga[:].rearrange("p i k j -> p (i k j)"))
+                else:
+                    view = c_raw[(n, g)][:].rearrange("p j (i k) -> p i j k", k=6)
+                    gb = stage.tile([P, 2 * BLK, 4], BF16, tag="grpb", name="gb", align_bytes=64)
+                    copy_on(False, gb[:, 0:BLK, :], view[:, :, :, 5])
+                    copy_on(
+                        n in W_ON_V,
+                        gb[:, BLK : 2 * BLK, :].rearrange("p (c i) t -> p c t i", i=4),
+                        w_raw[(n, g)][:].rearrange("p t (c i) -> p c t i", i=4),
+                    )
+                    tiles.append(gb[:].rearrange("p c t -> p (c t)"))
+            grouped[unit] = tiles
+
+        def quantise(unit):
+            pool = codes_a if unit[0] == "A" else codes_b
+            pairs = []
+            for g in range(NG):
+                cd = pool.tile([P, 512], U32, tag="codes", name="cd", align_bytes=64)
+                sc = pool.tile([P, 512], U8, tag="scales", name="sc", align_bytes=64)
+                nc.vector.quantize_mx(out=cd[:].bitcast(E4M3X4), scales=sc[:], in_=grouped[unit][g])
+                pairs.append((cd, sc))
+            opnd[unit] = pairs
+
+        def multiply(unit):
+            tiles = []
+            for bt in range(NB):
+                bank = psum.tile([P, 512], F32, tag="bank", name="bank")
+                for g in range(NG):
+                    sl = slice((g * NB + bt) * P, (g * NB + bt + 1) * P)
+                    nc.tensor.matmul_mx(
+                        out=bank[:],
+                        lhsT=g_codes[:, sl].bitcast(E5M2X4),
+                        lhsT_scale=g_scales[:, sl],
+                        rhs=opnd[unit][g][0][:].bitcast(E4M3X4),
+                        rhs_scale=opnd[unit][g][1][:],
+                        start=(g == 0),
+                        stop=(g == NG - 1),
+                    )
+                tiles.append(bank)
+            banks[unit] = tiles
+
+        def stt(dst, in0, scalar, in1, op0, op1):
+            nc.vector.scalar_tensor_tensor(out=dst, in0=in0, scalar=scalar, in1=in1, op0=op0, op1=op1)
+
+        def leave_psum(unit):
+            kind, n = unit
+            if kind == "B":
+                th, ut, sq = facs[n]
+                p5 = work.tile([P, NB, BLK], F32, tag="p5", name="p5")
+                p0 = work.tile([P, NB, BLK], F32, tag="p0", name="p0")
+                ob = work.tile([P, NB, BLK], F32, tag="ob", name="ob")
+                for bt in range(NB):
+                    pb = banks[unit][bt]
+                    stt(p5[:, bt, :], sq[:, bt, :], ks * beta, pb[:, 0:BLK], ALU.add, ALU.mult)
+                    stt(p0[:, bt, :], pb[:, BLK:512], -1.0, nf0[n][:, bt, :], ALU.mult, ALU.mult)
+                res[unit] = (p5, p0, ob)
+            else:
+                blk, h = divmod(n, 2)
+                hs = slice(TILE_I * h, TILE_I * (h + 1))
+                th, ut, sq = facs[blk]
+                a1 = work2.tile([P, NB, TILE_I], F32, tag="a1", name="a1")
+                a2 = work2.tile([P, NB, TILE_I], F32, tag="a2", name="a2")
+                for bt in range(NB):
+                    hv = banks[unit][bt][:].rearrange("p (i k) -> p k i", k=4)
+                    stt(a1[:, bt, :], ut[:, bt, hs], lam * r3, hv[:, 2, :], ALU.add, ALU.mult)
+                    stt(a2[:, bt, :], ut[:, bt, hs], lam * r4, hv[:, 3, :], ALU.add, ALU.mult)
+                    stt(a1[:, bt, :], hv[:, 0, :], 2.0 * lam / c31, a1[:, bt, :], ALU.mult, ALU.add)
+                    stt(a2[:, bt, :], hv[:, 1, :], lam * c2 / c41, a2[:, bt, :], ALU.mult, ALU.add)
+                res[unit] = (a1, a2)
+
+        def side(n):
+            return nc.vector if (LAST_ON_V and n == 2 * NBLK - 1) else nc.gpsimd
+
+        def join_first(n):
+            blk, h = divmod(n, 2)
+            hs = slice(TILE_I * h, TILE_I * (h + 1))
+            a1, a2 = res[("A", n)]
+            side(n).tensor_tensor(out=a2[:], in0=a2[:], in1=facs[blk][0][:, :, hs], op=ALU.mult)
+            side(n).tensor_tensor(out=a1[:], in0=a1[:], in1=res[("B", blk)][0][:, :, hs], op=ALU.add)
+
+        def join_second(n):
+            blk, h = divmod(n, 2)
+            hs = slice(TILE_I * h, TILE_I * (h + 1))
+            a1, a2 = res[("A", n)]
+            stt(a1[:], a2[:], c41 / c31, a1[:], ALU.mult, ALU.add)
+            stt(a1[:], facs[blk][1][:, :, hs], -lam, a1[:], ALU.add, ALU.mult)
+
+        def finish(n):
+            blk, h = divmod(n, 2)
+            hs = slice(TILE_I * h, TILE_I * (h + 1))
+            a1, a2 = res[("A", n)]
+            p5, p0, ob = res[("B", blk)]
+            side(n).tensor_tensor(out=ob[:, :, hs], in0=p0[:, :, hs], in1=a1[:], op=ALU.subtract)
+            if blk == NBLK - 1:
+                nc.sync.dma_start(
+                    out=out_v[:, :, BLK * blk + TILE_I * h : BLK * blk + TILE_I * (h + 1)], in_=ob[:, :, hs]
+                )
+            elif h == 1:
+                nc.gpsimd.dma_start(out=out_v[:, :, BLK * blk : BLK * (blk + 1)], in_=ob[:])
+
+        left = []
+        joined1 = []
+        joined2 = []
+        b_done = set()
+        for m in range(-LEAD_R, n_units + 3):
+            for n in joined2:
+                finish(n)
+            joined2 = []
+            for n in joined1:
+                join_second(n)
+                joined2.append(n)
+            joined1 = []
+            r = m + LEAD_R
+            if 0 <= r < n_units:
+                if r % 3 == 0:
+                    activations(r // 3)
+                regroup(units[r])
+                if r % 3 == 2 and r // 3 + 1 < NBLK:
+                    load_block(r // 3 + 1)
+            if m == -1:
+                silu_grad_v((2, 3), s_second)
+            if 0 <= m < n_units:
+                leave_psum(units[m])
+                if units[m][0] == "B":
+                    b_done.add(units[m][1])
+                else:
+                    left.append(units[m][1])
+            still = []
+            for n in left:
+                if n // 2 in b_done:
+                    join_first(n)
+                    joined1.append(n)
+                else:
+                    still.append(n)
+            left = still
+            if 0 <= m + LEAD_Q < n_units:
+                quantise(units[m + LEAD_Q])
+            if 0 <= m + LEAD_M < n_units:
+                multiply(units[m + LEAD_M])

@@ -28,12 +28,11 @@ FLOPS = 2 * (DEGREE + 1) * BATCH * IN_F * OUT_F
 BYTES = 2 * (2 * BATCH * IN_F + IN_F * OUT_F * (DEGREE + 1)) + 4 * BATCH * IN_F
 
 PIN = True
-V_TILES = (0,)
-W_ON_V = (0, 1, 2, 3)
-LEAD_R = 3
-LEAD_Q = 2
-LEAD_M = 1
-LAST_ON_V = False
+A_ON_V = ((0, 0), (0, 1))
+W_ON_V = (0,)
+C5_ON_V = ()
+LAST_ON_V = True
+GP_OPS = True
 
 
 def derivative_polynomials():
@@ -72,19 +71,21 @@ def tile_jacobikanlinear_kernel(tc, x, base_weight, jacobi_coeffs, bias, grad_ou
         else:
             nc.scalar.copy(out=dst, in_=src)
 
+    def stt(dst, in0, scalar, in1, op0, op1):
+        nc.vector.scalar_tensor_tensor(out=dst, in0=in0, scalar=scalar, in1=in1, op0=op0, op1=op1)
+
     with ExitStack() as ctx:
         if PIN:
             ctx.enter_context(tc.manual_schedule())
         keep = ctx.enter_context(tc.tile_pool(name="keep", bufs=1))
         ring = ctx.enter_context(tc.tile_pool(name="ring", bufs=4))
         wring = ctx.enter_context(tc.tile_pool(name="wring", bufs=4))
-        stage = ctx.enter_context(tc.tile_pool(name="stage", bufs=4))
-        codes_a = ctx.enter_context(tc.tile_pool(name="codes_a", bufs=6))
+        stage_a = ctx.enter_context(tc.tile_pool(name="stage_a", bufs=3))
+        stage_b = ctx.enter_context(tc.tile_pool(name="stage_b", bufs=3))
+        codes_a = ctx.enter_context(tc.tile_pool(name="codes_a", bufs=4))
         codes_b = ctx.enter_context(tc.tile_pool(name="codes_b", bufs=4))
-        sig = ctx.enter_context(tc.tile_pool(name="sig", bufs=2))
-        fac = ctx.enter_context(tc.tile_pool(name="fac", bufs=3))
+        fac3 = ctx.enter_context(tc.tile_pool(name="fac3", bufs=3))
         work = ctx.enter_context(tc.tile_pool(name="work", bufs=2))
-        work2 = ctx.enter_context(tc.tile_pool(name="work2", bufs=3))
         psum = ctx.enter_context(tc.psum_pool(name="psum", bufs=8))
 
         ident = keep.tile([P, P], F32, name="ident")
@@ -98,6 +99,14 @@ def tile_jacobikanlinear_kernel(tc, x, base_weight, jacobi_coeffs, bias, grad_ou
 
         c_raw = {}
         w_raw = {}
+        nf0 = {}
+        s_t = {}
+        facs = {}
+        grp_a = {}
+        grp_b = {}
+        opnd = {}
+        banks = {}
+        res = {}
 
         def load_block(blk):
             for g in range(NG):
@@ -119,34 +128,147 @@ def tile_jacobikanlinear_kernel(tc, x, base_weight, jacobi_coeffs, bias, grad_ou
                 )
                 w_raw[(blk, g)] = raw
 
-        load_block(0)
-
-        nf0 = {}
+        def sigmoid(blk):
+            cs = slice(BLK * blk, BLK * (blk + 1))
+            s_t[blk] = work.tile([P, NB, BLK], F32, tag=("p5" if blk < 2 else "p0"), name="s_sb")
+            nc.scalar.activation(out=s_t[blk][:], in_=x_sb[:, :, cs], func=ACT.Sigmoid)
 
         def silu_grad(blks):
-            s_t = {}
-            for blk in blks:
-                cs = slice(BLK * blk, BLK * (blk + 1))
-                s_t[blk] = sig.tile([P, NB, BLK], F32, tag="s", name="s_sb")
-                nc.scalar.activation(out=s_t[blk][:], in_=x_sb[:, :, cs], func=ACT.Sigmoid)
-            return s_t
-
-        def silu_grad_v(blks, s_t):
             for blk in blks:
                 cs = slice(BLK * blk, BLK * (blk + 1))
                 nf0[blk] = keep.tile([P, NB, BLK], F32, name="nf0_%d" % blk)
-                nc.vector.scalar_tensor_tensor(
-                    out=nf0[blk][:], in0=s_t[blk][:], scalar=-1.0, in1=x_sb[:, :, cs], op0=ALU.add, op1=ALU.mult
-                )
+                stt(nf0[blk][:], s_t[blk][:], -1.0, x_sb[:, :, cs], ALU.add, ALU.mult)
             for blk in blks:
-                nc.vector.scalar_tensor_tensor(
-                    out=nf0[blk][:], in0=nf0[blk][:], scalar=-1.0, in1=s_t[blk][:], op0=ALU.add, op1=ALU.mult
+                stt(nf0[blk][:], nf0[blk][:], -1.0, s_t[blk][:], ALU.add, ALU.mult)
+
+        def activations(blk):
+            cs = slice(BLK * blk, BLK * (blk + 1))
+            th = fac3.tile([P, NB, BLK], F32, tag="th", name="th")
+            nc.scalar.activation(out=th[:], in_=x_sb[:, :, cs], func=ACT.Tanh)
+            ut = fac3.tile([P, NB, BLK], F32, tag="ut", name="ut")
+            nc.scalar.activation(out=ut[:], in_=th[:], func=ACT.Square, scale=math.sqrt(lam))
+            sq = work.tile([P, NB, BLK], F32, tag="sq", name="sq")
+            nc.scalar.activation(
+                out=sq[:], in_=ut[:], func=ACT.Square, scale=math.sqrt(ks) / lam, bias=math.sqrt(ks) * alpha
+            )
+            facs[blk] = (th, ut, sq)
+
+        def regroup_b(blk):
+            for g in range(NG):
+                view = c_raw[(blk, g)][:].rearrange("p j (i k) -> p i j k", k=6)
+                gb = stage_b.tile([P, 2 * BLK, 4], BF16, tag="grpb", name="gb", align_bytes=64)
+                copy_on(blk in C5_ON_V, gb[:, 0:BLK, :], view[:, :, :, 5])
+                copy_on(
+                    blk in W_ON_V,
+                    gb[:, BLK : 2 * BLK, :].rearrange("p (c i) t -> p c t i", i=4),
+                    w_raw[(blk, g)][:].rearrange("p t (c i) -> p c t i", i=4),
                 )
+                grp_b[(blk, g)] = gb
 
-        s_first = silu_grad((0, 1))
-        silu_grad_v((0, 1), s_first)
-        s_second = silu_grad((2, 3))
+        def regroup_a(blk, g):
+            view = c_raw[(blk, g)][:].rearrange("p j (i k) -> p i j k", k=6)
+            ga = stage_a.tile([P, 4, BLK, 4], BF16, tag="grpa", name="ga", align_bytes=64)
+            copy_on((blk, g) in A_ON_V, ga[:].rearrange("p k i j -> p i j k"), view[:, :, :, 1:5])
+            grp_a[(blk, g)] = ga
 
+        def quantise_b(blk):
+            for g in range(NG):
+                cd = codes_b.tile([P, 512], U32, tag="codes", name="cdb", align_bytes=64)
+                sc = codes_b.tile([P, 512], U8, tag="scales", name="scb", align_bytes=64)
+                nc.vector.quantize_mx(
+                    out=cd[:].bitcast(E4M3X4), scales=sc[:], in_=grp_b[(blk, g)][:].rearrange("p c t -> p (c t)")
+                )
+                opnd[("B", blk, g)] = (cd[:], sc[:])
+
+        def quantise_a(blk, g):
+            cd = codes_a.tile([P, 1024], U32, tag="codes", name="cda", align_bytes=64)
+            sc = codes_a.tile([P, 1024], U8, tag="scales", name="sca", align_bytes=64)
+            nc.vector.quantize_mx(
+                out=cd[:].bitcast(E4M3X4), scales=sc[:], in_=grp_a[(blk, g)][:].rearrange("p k i j -> p (k i j)")
+            )
+            opnd[("Y", blk, g)] = (cd[:, 0:512], sc[:, 0:512])
+            opnd[("X", blk, g)] = (cd[:, 512:1024], sc[:, 512:1024])
+
+        def multiply(kind, blk):
+            tiles = []
+            for bt in range(NB):
+                bank = psum.tile([P, 512], F32, tag="bank", name="bank")
+                for g in range(NG):
+                    sl = slice((g * NB + bt) * P, (g * NB + bt + 1) * P)
+                    cd, sc = opnd[(kind, blk, g)]
+                    nc.tensor.matmul_mx(
+                        out=bank[:],
+                        lhsT=g_codes[:, sl].bitcast(E5M2X4),
+                        lhsT_scale=g_scales[:, sl],
+                        rhs=cd.bitcast(E4M3X4),
+                        rhs_scale=sc,
+                        start=(g == 0),
+                        stop=(g == NG - 1),
+                    )
+                tiles.append(bank)
+            banks[(kind, blk)] = tiles
+
+        def leave_b(blk):
+            th, ut, sq = facs[blk]
+            p5 = work.tile([P, NB, BLK], F32, tag="p5", name="p5")
+            p0 = work.tile([P, NB, BLK], F32, tag="p0", name="p0")
+            for bt in range(NB):
+                pb = banks[("B", blk)][bt]
+                stt(p5[:, bt, :], sq[:, bt, :], ks * beta, pb[:, 0:BLK], ALU.add, ALU.mult)
+                stt(p0[:, bt, :], pb[:, BLK:512], -1.0, nf0[blk][:, bt, :], ALU.mult, ALU.mult)
+            res[("B", blk)] = (p5, p0)
+
+        def leave_x(blk):
+            th, ut, sq = facs[blk]
+            a1 = work.tile([P, NB, BLK], F32, tag="a1", name="a1")
+            a2 = work.tile([P, NB, BLK], F32, tag="a2", name="a2")
+            for bt in range(NB):
+                px = banks[("X", blk)][bt]
+                stt(a1[:, bt, :], ut[:, bt, :], lam * r3, px[:, 0:BLK], ALU.add, ALU.mult)
+                stt(a2[:, bt, :], ut[:, bt, :], lam * r4, px[:, BLK:512], ALU.add, ALU.mult)
+            res[("A", blk)] = (a1, a2)
+
+        def leave_y(blk):
+            a1, a2 = res[("A", blk)]
+            for bt in range(NB):
+                py = banks[("Y", blk)][bt]
+                stt(a1[:, bt, :], py[:, 0:BLK], 2.0 * lam / c31, a1[:, bt, :], ALU.mult, ALU.add)
+                stt(a2[:, bt, :], py[:, BLK:512], lam * c2 / c41, a2[:, bt, :], ALU.mult, ALU.add)
+
+        def side(blk):
+            if not GP_OPS or (LAST_ON_V and blk == NBLK - 1):
+                return nc.vector
+            return nc.gpsimd
+
+        def join_first(blk):
+            a1, a2 = res[("A", blk)]
+            side(blk).tensor_tensor(out=a2[:], in0=a2[:], in1=facs[blk][0][:], op=ALU.mult)
+            side(blk).tensor_tensor(out=a1[:], in0=a1[:], in1=res[("B", blk)][0][:], op=ALU.add)
+
+        def join_second(blk):
+            a1, a2 = res[("A", blk)]
+            stt(a1[:], a2[:], c41 / c31, a1[:], ALU.mult, ALU.add)
+            stt(a1[:], facs[blk][1][:], -lam, a1[:], ALU.add, ALU.mult)
+
+        def finish(blk):
+            a1, a2 = res[("A", blk)]
+            p5, p0 = res[("B", blk)]
+            side(blk).tensor_tensor(out=a2[:], in0=p0[:], in1=a1[:], op=ALU.subtract)
+            queue = nc.sync if blk == NBLK - 1 else nc.gpsimd
+            queue.dma_start(out=out_v[:, :, BLK * blk : BLK * (blk + 1)], in_=a2[:])
+
+        def prepare(blk):
+            activations(blk)
+            regroup_b(blk)
+            for g in range(NG):
+                regroup_a(blk, g)
+            if blk + 1 < NBLK:
+                load_block(blk + 1)
+
+        load_block(0)
+        for blk in range(NBLK):
+            sigmoid(blk)
+        silu_grad((0, 1))
         g32 = g_sb[:].bitcast(F32).rearrange("p n (g w u) -> p n g w u", g=NG, u=2)
         g_grp32 = g_grp[:].bitcast(F32).rearrange("p (s b u) -> p s b u", s=NG * NB, u=2)
         for pr in range(NG * NB // 2):
@@ -162,178 +284,34 @@ def tile_jacobikanlinear_kernel(tc, x, base_weight, jacobi_coeffs, bias, grad_ou
         g_scales = keep.tile([P, NG * NB * P], U8, name="g_scales", align_bytes=64)
         nc.vector.quantize_mx(out=g_codes[:].bitcast(E5M2X4), scales=g_scales[:], in_=g_grp[:])
 
-        units = []
+        prepare(0)
+        quantise_b(0)
+        multiply("B", 0)
+        silu_grad((2, 3))
+        for g in range(NG):
+            quantise_a(0, g)
+        multiply("X", 0)
+
         for blk in range(NBLK):
-            units.extend([("A", 2 * blk), ("B", blk), ("A", 2 * blk + 1)])
-        n_units = len(units)
-
-        grouped = {}
-        opnd = {}
-        banks = {}
-        facs = {}
-        res = {}
-
-        def activations(blk):
-            cs = slice(BLK * blk, BLK * (blk + 1))
-            th = fac.tile([P, NB, BLK], F32, tag="th", name="th")
-            nc.scalar.activation(out=th[:], in_=x_sb[:, :, cs], func=ACT.Tanh)
-            ut = fac.tile([P, NB, BLK], F32, tag="ut", name="ut")
-            nc.scalar.activation(out=ut[:], in_=th[:], func=ACT.Square, scale=math.sqrt(lam))
-            sq = fac.tile([P, NB, BLK], F32, tag="sq", name="sq")
-            nc.scalar.activation(
-                out=sq[:], in_=ut[:], func=ACT.Square, scale=math.sqrt(ks) / lam, bias=math.sqrt(ks) * alpha
-            )
-            facs[blk] = (th, ut, sq)
-
-        def regroup(unit):
-            kind, n = unit
-            tiles = []
-            for g in range(NG):
-                if kind == "A":
-                    blk, h = divmod(n, 2)
-                    view = c_raw[(blk, g)][:].rearrange("p j (i k) -> p i j k", k=6)
-                    ga = stage.tile([P, TILE_I, 4, 4], BF16, tag="grpa", name="ga", align_bytes=64)
-                    copy_on(
-                        n in V_TILES,
-                        ga[:].rearrange("p i k j -> p i j k"),
-                        view[:, TILE_I * h : TILE_I * (h + 1), :, 1:5],
-                    )
-                    tiles.append(ga[:].rearrange("p i k j -> p (i k j)"))
-                else:
-                    view = c_raw[(n, g)][:].rearrange("p j (i k) -> p i j k", k=6)
-                    gb = stage.tile([P, 2 * BLK, 4], BF16, tag="grpb", name="gb", align_bytes=64)
-                    copy_on(False, gb[:, 0:BLK, :], view[:, :, :, 5])
-                    copy_on(
-                        n in W_ON_V,
-                        gb[:, BLK : 2 * BLK, :].rearrange("p (c i) t -> p c t i", i=4),
-                        w_raw[(n, g)][:].rearrange("p t (c i) -> p c t i", i=4),
-                    )
-                    tiles.append(gb[:].rearrange("p c t -> p (c t)"))
-            grouped[unit] = tiles
-
-        def quantise(unit):
-            pool = codes_a if unit[0] == "A" else codes_b
-            pairs = []
-            for g in range(NG):
-                cd = pool.tile([P, 512], U32, tag="codes", name="cd", align_bytes=64)
-                sc = pool.tile([P, 512], U8, tag="scales", name="sc", align_bytes=64)
-                nc.vector.quantize_mx(out=cd[:].bitcast(E4M3X4), scales=sc[:], in_=grouped[unit][g])
-                pairs.append((cd, sc))
-            opnd[unit] = pairs
-
-        def multiply(unit):
-            tiles = []
-            for bt in range(NB):
-                bank = psum.tile([P, 512], F32, tag="bank", name="bank")
+            more = blk + 1 < NBLK
+            if more:
+                prepare(blk + 1)
+            leave_b(blk)
+            multiply("Y", blk)
+            if more:
+                quantise_b(blk + 1)
+            leave_x(blk)
+            if more:
+                multiply("B", blk + 1)
+            if blk > 0:
+                join_second(blk - 1)
+                finish(blk - 1)
+            if more:
                 for g in range(NG):
-                    sl = slice((g * NB + bt) * P, (g * NB + bt + 1) * P)
-                    nc.tensor.matmul_mx(
-                        out=bank[:],
-                        lhsT=g_codes[:, sl].bitcast(E5M2X4),
-                        lhsT_scale=g_scales[:, sl],
-                        rhs=opnd[unit][g][0][:].bitcast(E4M3X4),
-                        rhs_scale=opnd[unit][g][1][:],
-                        start=(g == 0),
-                        stop=(g == NG - 1),
-                    )
-                tiles.append(bank)
-            banks[unit] = tiles
-
-        def stt(dst, in0, scalar, in1, op0, op1):
-            nc.vector.scalar_tensor_tensor(out=dst, in0=in0, scalar=scalar, in1=in1, op0=op0, op1=op1)
-
-        def leave_psum(unit):
-            kind, n = unit
-            if kind == "B":
-                th, ut, sq = facs[n]
-                p5 = work.tile([P, NB, BLK], F32, tag="p5", name="p5")
-                p0 = work.tile([P, NB, BLK], F32, tag="p0", name="p0")
-                ob = work.tile([P, NB, BLK], F32, tag="ob", name="ob")
-                for bt in range(NB):
-                    pb = banks[unit][bt]
-                    stt(p5[:, bt, :], sq[:, bt, :], ks * beta, pb[:, 0:BLK], ALU.add, ALU.mult)
-                    stt(p0[:, bt, :], pb[:, BLK:512], -1.0, nf0[n][:, bt, :], ALU.mult, ALU.mult)
-                res[unit] = (p5, p0, ob)
-            else:
-                blk, h = divmod(n, 2)
-                hs = slice(TILE_I * h, TILE_I * (h + 1))
-                th, ut, sq = facs[blk]
-                a1 = work2.tile([P, NB, TILE_I], F32, tag="a1", name="a1")
-                a2 = work2.tile([P, NB, TILE_I], F32, tag="a2", name="a2")
-                for bt in range(NB):
-                    hv = banks[unit][bt][:].rearrange("p (i k) -> p k i", k=4)
-                    stt(a1[:, bt, :], ut[:, bt, hs], lam * r3, hv[:, 2, :], ALU.add, ALU.mult)
-                    stt(a2[:, bt, :], ut[:, bt, hs], lam * r4, hv[:, 3, :], ALU.add, ALU.mult)
-                    stt(a1[:, bt, :], hv[:, 0, :], 2.0 * lam / c31, a1[:, bt, :], ALU.mult, ALU.add)
-                    stt(a2[:, bt, :], hv[:, 1, :], lam * c2 / c41, a2[:, bt, :], ALU.mult, ALU.add)
-                res[unit] = (a1, a2)
-
-        def side(n):
-            return nc.vector if (LAST_ON_V and n == 2 * NBLK - 1) else nc.gpsimd
-
-        def join_first(n):
-            blk, h = divmod(n, 2)
-            hs = slice(TILE_I * h, TILE_I * (h + 1))
-            a1, a2 = res[("A", n)]
-            side(n).tensor_tensor(out=a2[:], in0=a2[:], in1=facs[blk][0][:, :, hs], op=ALU.mult)
-            side(n).tensor_tensor(out=a1[:], in0=a1[:], in1=res[("B", blk)][0][:, :, hs], op=ALU.add)
-
-        def join_second(n):
-            blk, h = divmod(n, 2)
-            hs = slice(TILE_I * h, TILE_I * (h + 1))
-            a1, a2 = res[("A", n)]
-            stt(a1[:], a2[:], c41 / c31, a1[:], ALU.mult, ALU.add)
-            stt(a1[:], facs[blk][1][:, :, hs], -lam, a1[:], ALU.add, ALU.mult)
-
-        def finish(n):
-            blk, h = divmod(n, 2)
-            hs = slice(TILE_I * h, TILE_I * (h + 1))
-            a1, a2 = res[("A", n)]
-            p5, p0, ob = res[("B", blk)]
-            side(n).tensor_tensor(out=ob[:, :, hs], in0=p0[:, :, hs], in1=a1[:], op=ALU.subtract)
-            if blk == NBLK - 1:
-                nc.sync.dma_start(
-                    out=out_v[:, :, BLK * blk + TILE_I * h : BLK * blk + TILE_I * (h + 1)], in_=ob[:, :, hs]
-                )
-            elif h == 1:
-                nc.gpsimd.dma_start(out=out_v[:, :, BLK * blk : BLK * (blk + 1)], in_=ob[:])
-
-        left = []
-        joined1 = []
-        joined2 = []
-        b_done = set()
-        for m in range(-LEAD_R, n_units + 3):
-            for n in joined2:
-                finish(n)
-            joined2 = []
-            for n in joined1:
-                join_second(n)
-                joined2.append(n)
-            joined1 = []
-            r = m + LEAD_R
-            if 0 <= r < n_units:
-                if r % 3 == 0:
-                    activations(r // 3)
-                regroup(units[r])
-                if r % 3 == 2 and r // 3 + 1 < NBLK:
-                    load_block(r // 3 + 1)
-            if m == -1:
-                silu_grad_v((2, 3), s_second)
-            if 0 <= m < n_units:
-                leave_psum(units[m])
-                if units[m][0] == "B":
-                    b_done.add(units[m][1])
-                else:
-                    left.append(units[m][1])
-            still = []
-            for n in left:
-                if n // 2 in b_done:
-                    join_first(n)
-                    joined1.append(n)
-                else:
-                    still.append(n)
-            left = still
-            if 0 <= m + LEAD_Q < n_units:
-                quantise(units[m + LEAD_Q])
-            if 0 <= m + LEAD_M < n_units:
-                multiply(units[m + LEAD_M])
+                    quantise_a(blk + 1, g)
+            leave_y(blk)
+            if more:
+                multiply("X", blk + 1)
+            join_first(blk)
+        join_second(NBLK - 1)
+        finish(NBLK - 1)

@@ -28,10 +28,9 @@ FLOPS = 2 * (DEGREE + 1) * BATCH * IN_F * OUT_F
 BYTES = 2 * (2 * BATCH * IN_F + IN_F * OUT_F * (DEGREE + 1)) + 4 * BATCH * IN_F
 
 PIN = True
-A_ON_V = ((0, 0), (0, 1))
-W_ON_V = (0,)
-C5_ON_V = ()
-LAST_ON_V = True
+V123 = ((0, 0), (0, 1))
+V45 = ((0, 1), (0, 0))
+VW = ((0, 1), (1, 0), (1, 1), (2, 0), (2, 1), (3, 0))
 GP_OPS = True
 
 
@@ -80,10 +79,9 @@ def tile_jacobikanlinear_kernel(tc, x, base_weight, jacobi_coeffs, bias, grad_ou
         keep = ctx.enter_context(tc.tile_pool(name="keep", bufs=1))
         ring = ctx.enter_context(tc.tile_pool(name="ring", bufs=4))
         wring = ctx.enter_context(tc.tile_pool(name="wring", bufs=4))
-        stage_a = ctx.enter_context(tc.tile_pool(name="stage_a", bufs=3))
-        stage_b = ctx.enter_context(tc.tile_pool(name="stage_b", bufs=3))
-        codes_a = ctx.enter_context(tc.tile_pool(name="codes_a", bufs=4))
-        codes_b = ctx.enter_context(tc.tile_pool(name="codes_b", bufs=4))
+        stage1 = ctx.enter_context(tc.tile_pool(name="stage1", bufs=3))
+        stage2 = ctx.enter_context(tc.tile_pool(name="stage2", bufs=3))
+        codes = ctx.enter_context(tc.tile_pool(name="codes", bufs=4))
         fac3 = ctx.enter_context(tc.tile_pool(name="fac3", bufs=3))
         work = ctx.enter_context(tc.tile_pool(name="work", bufs=2))
         psum = ctx.enter_context(tc.psum_pool(name="psum", bufs=8))
@@ -101,9 +99,9 @@ def tile_jacobikanlinear_kernel(tc, x, base_weight, jacobi_coeffs, bias, grad_ou
         w_raw = {}
         nf0 = {}
         s_t = {}
+        y_t = {}
         facs = {}
-        grp_a = {}
-        grp_b = {}
+        grp = {}
         opnd = {}
         banks = {}
         res = {}
@@ -128,19 +126,6 @@ def tile_jacobikanlinear_kernel(tc, x, base_weight, jacobi_coeffs, bias, grad_ou
                 )
                 w_raw[(blk, g)] = raw
 
-        def sigmoid(blk):
-            cs = slice(BLK * blk, BLK * (blk + 1))
-            s_t[blk] = work.tile([P, NB, BLK], F32, tag=("p5" if blk < 2 else "p0"), name="s_sb")
-            nc.scalar.activation(out=s_t[blk][:], in_=x_sb[:, :, cs], func=ACT.Sigmoid)
-
-        def silu_grad(blks):
-            for blk in blks:
-                cs = slice(BLK * blk, BLK * (blk + 1))
-                nf0[blk] = keep.tile([P, NB, BLK], F32, name="nf0_%d" % blk)
-                stt(nf0[blk][:], s_t[blk][:], -1.0, x_sb[:, :, cs], ALU.add, ALU.mult)
-            for blk in blks:
-                stt(nf0[blk][:], nf0[blk][:], -1.0, s_t[blk][:], ALU.add, ALU.mult)
-
         def activations(blk):
             cs = slice(BLK * blk, BLK * (blk + 1))
             th = fac3.tile([P, NB, BLK], F32, tag="th", name="th")
@@ -153,41 +138,36 @@ def tile_jacobikanlinear_kernel(tc, x, base_weight, jacobi_coeffs, bias, grad_ou
             )
             facs[blk] = (th, ut, sq)
 
-        def regroup_b(blk):
+        def regroup(blk):
             for g in range(NG):
                 view = c_raw[(blk, g)][:].rearrange("p j (i k) -> p i j k", k=6)
-                gb = stage_b.tile([P, 2 * BLK, 4], BF16, tag="grpb", name="gb", align_bytes=64)
-                copy_on(blk in C5_ON_V, gb[:, 0:BLK, :], view[:, :, :, 5])
+                t1 = stage1.tile([P, 4, BLK, 4], BF16, tag="t1", name="t1", align_bytes=64)
+                t2 = stage2.tile([P, 2, BLK, 4], BF16, tag="t2", name="t2", align_bytes=64)
+                copy_on((blk, g) in V123, t1[:, 0:3, :, :].rearrange("p k i j -> p i j k"), view[:, :, :, 1:4])
                 copy_on(
-                    blk in W_ON_V,
-                    gb[:, BLK : 2 * BLK, :].rearrange("p (c i) t -> p c t i", i=4),
+                    (blk, g) in VW,
+                    t1[:, 3, :, :].rearrange("p (c i) t -> p c t i", i=4),
                     w_raw[(blk, g)][:].rearrange("p t (c i) -> p c t i", i=4),
                 )
-                grp_b[(blk, g)] = gb
+                copy_on((blk, g) in V45, t2[:].rearrange("p k i j -> p i j k"), view[:, :, :, 4:6])
+                grp[(blk, g)] = (t1, t2)
 
-        def regroup_a(blk, g):
-            view = c_raw[(blk, g)][:].rearrange("p j (i k) -> p i j k", k=6)
-            ga = stage_a.tile([P, 4, BLK, 4], BF16, tag="grpa", name="ga", align_bytes=64)
-            copy_on((blk, g) in A_ON_V, ga[:].rearrange("p k i j -> p i j k"), view[:, :, :, 1:5])
-            grp_a[(blk, g)] = ga
-
-        def quantise_b(blk):
+        def quantise(blk):
             for g in range(NG):
-                cd = codes_b.tile([P, 512], U32, tag="codes", name="cdb", align_bytes=64)
-                sc = codes_b.tile([P, 512], U8, tag="scales", name="scb", align_bytes=64)
+                cd = codes.tile([P, 1024], U32, tag="codes1", name="cd1", align_bytes=64)
+                sc = codes.tile([P, 1024], U8, tag="scales1", name="sc1", align_bytes=64)
                 nc.vector.quantize_mx(
-                    out=cd[:].bitcast(E4M3X4), scales=sc[:], in_=grp_b[(blk, g)][:].rearrange("p c t -> p (c t)")
+                    out=cd[:].bitcast(E4M3X4), scales=sc[:], in_=grp[(blk, g)][0][:].rearrange("p k i j -> p (k i j)")
                 )
-                opnd[("B", blk, g)] = (cd[:], sc[:])
-
-        def quantise_a(blk, g):
-            cd = codes_a.tile([P, 1024], U32, tag="codes", name="cda", align_bytes=64)
-            sc = codes_a.tile([P, 1024], U8, tag="scales", name="sca", align_bytes=64)
-            nc.vector.quantize_mx(
-                out=cd[:].bitcast(E4M3X4), scales=sc[:], in_=grp_a[(blk, g)][:].rearrange("p k i j -> p (k i j)")
-            )
-            opnd[("Y", blk, g)] = (cd[:, 0:512], sc[:, 0:512])
-            opnd[("X", blk, g)] = (cd[:, 512:1024], sc[:, 512:1024])
+                opnd[("Y", blk, g)] = (cd[:, 0:512], sc[:, 0:512])
+                opnd[("Z", blk, g)] = (cd[:, 512:1024], sc[:, 512:1024])
+            for g in range(NG):
+                cd = codes.tile([P, 512], U32, tag="codes2", name="cd2", align_bytes=64)
+                sc = codes.tile([P, 512], U8, tag="scales2", name="sc2", align_bytes=64)
+                nc.vector.quantize_mx(
+                    out=cd[:].bitcast(E4M3X4), scales=sc[:], in_=grp[(blk, g)][1][:].rearrange("p k i j -> p (k i j)")
+                )
+                opnd[("X", blk, g)] = (cd[:], sc[:])
 
         def multiply(kind, blk):
             tiles = []
@@ -208,67 +188,67 @@ def tile_jacobikanlinear_kernel(tc, x, base_weight, jacobi_coeffs, bias, grad_ou
                 tiles.append(bank)
             banks[(kind, blk)] = tiles
 
-        def leave_b(blk):
+        def leave_z(blk):
             th, ut, sq = facs[blk]
-            p5 = work.tile([P, NB, BLK], F32, tag="p5", name="p5")
+            a1 = work.tile([P, NB, BLK], F32, tag="a1", name="a1")
             p0 = work.tile([P, NB, BLK], F32, tag="p0", name="p0")
             for bt in range(NB):
-                pb = banks[("B", blk)][bt]
-                stt(p5[:, bt, :], sq[:, bt, :], ks * beta, pb[:, 0:BLK], ALU.add, ALU.mult)
-                stt(p0[:, bt, :], pb[:, BLK:512], -1.0, nf0[blk][:, bt, :], ALU.mult, ALU.mult)
-            res[("B", blk)] = (p5, p0)
+                pz = banks[("Z", blk)][bt]
+                stt(a1[:, bt, :], ut[:, bt, :], lam * r3, pz[:, 0:BLK], ALU.add, ALU.mult)
+                stt(p0[:, bt, :], pz[:, BLK:512], -1.0, nf0[blk][:, bt, :], ALU.mult, ALU.mult)
+            res[blk] = [a1, p0]
 
         def leave_x(blk):
             th, ut, sq = facs[blk]
-            a1 = work.tile([P, NB, BLK], F32, tag="a1", name="a1")
             a2 = work.tile([P, NB, BLK], F32, tag="a2", name="a2")
+            p5 = work.tile([P, NB, BLK], F32, tag="p5", name="p5")
             for bt in range(NB):
                 px = banks[("X", blk)][bt]
-                stt(a1[:, bt, :], ut[:, bt, :], lam * r3, px[:, 0:BLK], ALU.add, ALU.mult)
-                stt(a2[:, bt, :], ut[:, bt, :], lam * r4, px[:, BLK:512], ALU.add, ALU.mult)
-            res[("A", blk)] = (a1, a2)
+                stt(a2[:, bt, :], ut[:, bt, :], lam * r4, px[:, 0:BLK], ALU.add, ALU.mult)
+                stt(p5[:, bt, :], sq[:, bt, :], ks * beta, px[:, BLK:512], ALU.add, ALU.mult)
+            res[blk].extend([a2, p5])
 
         def leave_y(blk):
-            a1, a2 = res[("A", blk)]
+            a1, p0, a2, p5 = res[blk]
             for bt in range(NB):
                 py = banks[("Y", blk)][bt]
                 stt(a1[:, bt, :], py[:, 0:BLK], 2.0 * lam / c31, a1[:, bt, :], ALU.mult, ALU.add)
                 stt(a2[:, bt, :], py[:, BLK:512], lam * c2 / c41, a2[:, bt, :], ALU.mult, ALU.add)
 
-        def side(blk):
-            if not GP_OPS or (LAST_ON_V and blk == NBLK - 1):
-                return nc.vector
-            return nc.gpsimd
+        def join_first(blk, eng, bs):
+            a1, p0, a2, p5 = res[blk]
+            eng.tensor_tensor(out=a2[:, bs, :], in0=a2[:, bs, :], in1=facs[blk][0][:, bs, :], op=ALU.mult)
+            eng.tensor_tensor(out=a1[:, bs, :], in0=a1[:, bs, :], in1=p5[:, bs, :], op=ALU.add)
 
-        def join_first(blk):
-            a1, a2 = res[("A", blk)]
-            side(blk).tensor_tensor(out=a2[:], in0=a2[:], in1=facs[blk][0][:], op=ALU.mult)
-            side(blk).tensor_tensor(out=a1[:], in0=a1[:], in1=res[("B", blk)][0][:], op=ALU.add)
+        def join_second(blk, bs):
+            a1, p0, a2, p5 = res[blk]
+            stt(a1[:, bs, :], a2[:, bs, :], c41 / c31, a1[:, bs, :], ALU.mult, ALU.add)
+            stt(a1[:, bs, :], facs[blk][1][:, bs, :], -lam, a1[:, bs, :], ALU.add, ALU.mult)
 
-        def join_second(blk):
-            a1, a2 = res[("A", blk)]
-            stt(a1[:], a2[:], c41 / c31, a1[:], ALU.mult, ALU.add)
-            stt(a1[:], facs[blk][1][:], -lam, a1[:], ALU.add, ALU.mult)
-
-        def finish(blk):
-            a1, a2 = res[("A", blk)]
-            p5, p0 = res[("B", blk)]
-            side(blk).tensor_tensor(out=a2[:], in0=p0[:], in1=a1[:], op=ALU.subtract)
-            queue = nc.sync if blk == NBLK - 1 else nc.gpsimd
-            queue.dma_start(out=out_v[:, :, BLK * blk : BLK * (blk + 1)], in_=a2[:])
+        def finish(blk, eng, queue, bs):
+            a1, p0, a2, p5 = res[blk]
+            eng.tensor_tensor(out=a2[:, bs, :], in0=p0[:, bs, :], in1=a1[:, bs, :], op=ALU.subtract)
+            queue.dma_start(out=out_v[:, bs, BLK * blk : BLK * (blk + 1)], in_=a2[:, bs, :])
 
         def prepare(blk):
             activations(blk)
-            regroup_b(blk)
-            for g in range(NG):
-                regroup_a(blk, g)
+            regroup(blk)
             if blk + 1 < NBLK:
                 load_block(blk + 1)
 
+        side = nc.gpsimd if GP_OPS else nc.vector
+        whole = slice(0, NB)
+
         load_block(0)
+        tags = ("a1", "p0", "a2", "p5")
         for blk in range(NBLK):
-            sigmoid(blk)
-        silu_grad((0, 1))
+            cs = slice(BLK * blk, BLK * (blk + 1))
+            s_t[blk] = work.tile([P, NB, BLK], F32, tag=tags[blk // 2], name="s_sb")
+            nc.scalar.activation(out=s_t[blk][:], in_=x_sb[:, :, cs], func=ACT.Sigmoid)
+        for blk in range(NBLK):
+            cs = slice(BLK * blk, BLK * (blk + 1))
+            y_t[blk] = work.tile([P, NB, BLK], F32, tag=tags[2 + blk // 2], name="y_sb")
+            nc.scalar.activation(out=y_t[blk][:], in_=x_sb[:, :, cs], func=ACT.Silu, scale=-1.0)
         g32 = g_sb[:].bitcast(F32).rearrange("p n (g w u) -> p n g w u", g=NG, u=2)
         g_grp32 = g_grp[:].bitcast(F32).rearrange("p (s b u) -> p s b u", s=NG * NB, u=2)
         for pr in range(NG * NB // 2):
@@ -283,35 +263,32 @@ def tile_jacobikanlinear_kernel(tc, x, base_weight, jacobi_coeffs, bias, grad_ou
         g_codes = keep.tile([P, NG * NB * P], U32, name="g_codes", align_bytes=64)
         g_scales = keep.tile([P, NG * NB * P], U8, name="g_scales", align_bytes=64)
         nc.vector.quantize_mx(out=g_codes[:].bitcast(E5M2X4), scales=g_scales[:], in_=g_grp[:])
+        for blk in range(NBLK):
+            nf0[blk] = keep.tile([P, NB, BLK], F32, name="nf0_%d" % blk)
+            stt(nf0[blk][:], y_t[blk][:], -1.0, s_t[blk][:], ALU.add, ALU.mult)
 
         prepare(0)
-        quantise_b(0)
-        multiply("B", 0)
-        silu_grad((2, 3))
-        for g in range(NG):
-            quantise_a(0, g)
+        quantise(0)
+        multiply("Z", 0)
         multiply("X", 0)
 
         for blk in range(NBLK):
             more = blk + 1 < NBLK
-            if more:
-                prepare(blk + 1)
-            leave_b(blk)
+            leave_z(blk)
             multiply("Y", blk)
-            if more:
-                quantise_b(blk + 1)
             leave_x(blk)
-            if more:
-                multiply("B", blk + 1)
             if blk > 0:
-                join_second(blk - 1)
-                finish(blk - 1)
-            if more:
-                for g in range(NG):
-                    quantise_a(blk + 1, g)
+                join_second(blk - 1, whole)
+                finish(blk - 1, side, nc.gpsimd, whole)
             leave_y(blk)
             if more:
+                join_first(blk, side, whole)
+                prepare(blk + 1)
+                quantise(blk + 1)
+                multiply("Z", blk + 1)
                 multiply("X", blk + 1)
-            join_first(blk)
-        join_second(NBLK - 1)
-        finish(NBLK - 1)
+        for half in range(2):
+            bs = slice(2 * half, 2 * half + 2)
+            join_first(NBLK - 1, nc.vector, bs)
+            join_second(NBLK - 1, bs)
+            finish(NBLK - 1, nc.vector, nc.sync, bs)

@@ -28,8 +28,8 @@ FLOPS = 2 * (DEGREE + 1) * BATCH * IN_F * OUT_F
 BYTES = 2 * (2 * BATCH * IN_F + IN_F * OUT_F * (DEGREE + 1)) + 4 * BATCH * IN_F
 
 PIN = True
-V123 = ((0, 0), (0, 1))
-V45 = ((0, 1), (0, 0))
+V123 = ((0, 0), (0, 1), (1, 0))
+V45 = ((0, 1), (0, 0), (2, 0))
 VW = ((0, 1), (1, 0), (1, 1), (2, 0), (2, 1), (3, 0))
 GP_OPS = True
 

@@ -28,9 +28,9 @@ FLOPS = 2 * (DEGREE + 1) * BATCH * IN_F * OUT_F
 BYTES = 2 * (2 * BATCH * IN_F + IN_F * OUT_F * (DEGREE + 1)) + 4 * BATCH * IN_F
 
 PIN = True
-V123 = ((0, 0), (0, 1), (1, 0))
-V45 = ((0, 1), (0, 0), (2, 0))
-VW = ((0, 1), (1, 0), (1, 1), (2, 0), (2, 1), (3, 0))
+V123 = ((0, 0), (0, 1))
+V45 = ()
+VW = ((0, 0), (0, 1), (1, 0), (1, 1), (3, 1))
 GP_OPS = True
 
 

@@ -29,8 +29,8 @@ BYTES = 2 * (2 * BATCH * IN_F + IN_F * OUT_F * (DEGREE + 1)) + 4 * BATCH * IN_F
 
 PIN = True
 V123 = ((0, 0), (0, 1))
-V45 = ()
-VW = ((0, 0), (0, 1), (1, 0), (1, 1), (3, 1))
+V45 = ((0, 1),)
+VW = ((0, 1), (1, 0), (1, 1), (2, 1), (3, 0))
 GP_OPS = True
 
 

@@ -29,8 +29,8 @@ BYTES = 2 * (2 * BATCH * IN_F + IN_F * OUT_F * (DEGREE + 1)) + 4 * BATCH * IN_F
 
 PIN = True
 V123 = ((0, 0), (0, 1))
-V45 = ((0, 1),)
-VW = ((0, 1), (1, 0), (1, 1), (2, 1), (3, 0))
+V45 = ((0, 1), (0, 0))
+VW = ((0, 1), (1, 0), (1, 1), (2, 0), (2, 1), (3, 0))
 GP_OPS = True
 
 
@@ -279,7 +279,7 @@ def tile_jacobikanlinear_kernel(tc, x, base_weight, jacobi_coeffs, bias, grad_ou
             leave_x(blk)
             if blk > 0:
                 join_second(blk - 1, whole)
-                finish(blk - 1, side, nc.gpsimd, whole)
+                finish(blk - 1, side, nc.sync, whole)
             leave_y(blk)
             if more:
                 join_first(blk, side, whole)

@@ -233,8 +233,8 @@ def tile_jacobikanlinear_kernel(tc, x, base_weight, jacobi_coeffs, bias, grad_ou
         def prepare(blk):
             activations(blk)
             regroup(blk)
-            if blk + 1 < NBLK:
-                load_block(blk + 1)
+            if blk + 2 < NBLK:
+                load_block(blk + 2)
 
         side = nc.gpsimd if GP_OPS else nc.vector
         whole = slice(0, NB)
@@ -263,6 +263,7 @@ def tile_jacobikanlinear_kernel(tc, x, base_weight, jacobi_coeffs, bias, grad_ou
         g_codes = keep.tile([P, NG * NB * P], U32, name="g_codes", align_bytes=64)
         g_scales = keep.tile([P, NG * NB * P], U8, name="g_scales", align_bytes=64)
         nc.vector.quantize_mx(out=g_codes[:].bitcast(E5M2X4), scales=g_scales[:], in_=g_grp[:])
+        load_block(1)
         for blk in range(NBLK):
             nf0[blk] = keep.tile([P, NB, BLK], F32, name="nf0_%d" % blk)
             stt(nf0[blk][:], y_t[blk][:], -1.0, s_t[blk][:], ALU.add, ALU.mult)

from contextlib import ExitStack
import math

import concourse.mybir as mybir
from concourse.masks import make_identity

F32 = mybir.dt.float32
BF16 = mybir.dt.bfloat16
U32 = mybir.dt.uint32
U8 = mybir.dt.uint8
E4M3X4 = mybir.dt.float8_e4m3fn_x4
E5M2X4 = mybir.dt.float8_e5m2_x4
ACT = mybir.ActivationFunctionType
ALU = mybir.AluOpType

P = 128
BATCH = 512
IN_F = 1024
OUT_F = 1024
DEGREE = 5
NB = BATCH // P
NG = OUT_F // 512
BLK = 256
NBLK = IN_F // BLK
TILE_I = 128

FLOPS = 2 * (DEGREE + 1) * BATCH * IN_F * OUT_F
BYTES = 2 * (2 * BATCH * IN_F + IN_F * OUT_F * (DEGREE + 1)) + 4 * BATCH * IN_F

PIN = True
V123 = ((0, 0), (0, 1))
V45 = ((0, 1), (0, 0))
VW = ((0, 1), (1, 0), (1, 1), (2, 0), (2, 1), (3, 0))
GP_OPS = True


def derivative_polynomials():
    polys = [[1.0], [0.0, 2.0]]
    for k in range(2, DEGREE + 1):
        a_k = k * (k + 2.0) / ((2.0 * k + 1.0) * (k + 1.0))
        b_k = k / (2.0 * k + 1.0)
        nxt = [0.0] + [a_k * c for c in polys[k - 1]]
        for n, c in enumerate(polys[k - 2]):
            nxt[n] -= b_k * c
        polys.append(nxt)
    return [[n * c for n, c in enumerate(p)][1:] for p in polys]


def tile_jacobikanlinear_kernel(tc, x, base_weight, jacobi_coeffs, bias, grad_out, out):
    nc = tc.nc
    q = derivative_polynomials()
    c2 = q[2][1]
    c30, c31 = q[3][0], q[3][2]
    c40, c41 = q[4][1], q[4][3]
    c50, c51, c52 = q[5][0], q[5][2], q[5][4]
    lam = math.sqrt(c31)
    r3 = c30 / c31
    r4 = c40 / c41
    alpha = c51 / (2.0 * c52)
    beta = c50 / c52 - alpha * alpha
    ks = lam * c52 / c31

    x_v = x.rearrange("(n p) i -> p n i", p=P)
    g_v = grad_out.rearrange("(n p) o -> p n o", p=P)
    out_v = out.rearrange("(n p) i -> p n i", p=P)

    def copy_on(on_vector, dst, src):
        if on_vector:
            nc.vector.tensor_copy(out=dst, in_=src)
        else:
            nc.scalar.copy(out=dst, in_=src)

    def stt(dst, in0, scalar, in1, op0, op1):
        nc.vector.scalar_tensor_tensor(out=dst, in0=in0, scalar=scalar, in1=in1, op0=op0, op1=op1)

    with ExitStack() as ctx:
        if PIN:
            ctx.enter_context(tc.manual_schedule())
        keep = ctx.enter_context(tc.tile_pool(name="keep", bufs=1))
        ring = ctx.enter_context(tc.tile_pool(name="ring", bufs=4))
        wring = ctx.enter_context(tc.tile_pool(name="wring", bufs=4))
        stage1 = ctx.enter_context(tc.tile_pool(name="stage1", bufs=3))
        stage2 = ctx.enter_context(tc.tile_pool(name="stage2", bufs=3))
        codes = ctx.enter_context(tc.tile_pool(name="codes", bufs=4))
        fac3 = ctx.enter_context(tc.tile_pool(name="fac3", bufs=3))
        work = ctx.enter_context(tc.tile_pool(name="work", bufs=2))
        psum = ctx.enter_context(tc.psum_pool(name="psum", bufs=8))

        ident = keep.tile([P, P], F32, name="ident")
        make_identity(nc, ident[:])

        x_sb = keep.tile([P, NB, IN_F], BF16, name="x_sb")
        nc.sync.dma_start(out=x_sb[:], in_=x_v)
        g_sb = ring.tile([P, NB, OUT_F], BF16, tag="stream", name="g_sb", align_bytes=64)
        nc.sync.dma_start(out=g_sb[:], in_=g_v)
        g_grp = ring.tile([P, 2 * NB * P * 4], BF16, tag="stream", name="g_grp", align_bytes=64)

        c_raw = {}
        w_raw = {}
        nf0 = {}
        s_t = {}
        y_t = {}
        facs = {}
        grp = {}
        opnd = {}
        banks = {}
        res = {}

        def load_block(blk):
            for g in range(NG):
                raw = ring.tile([P, 4, BLK * 6], BF16, tag="stream", name="c_raw", align_bytes=64)
                nc.sync.dma_start(
                    out=raw[:],
                    in_=jacobi_coeffs[512 * g : 512 * (g + 1), BLK * blk : BLK * (blk + 1), :].rearrange(
                        "(p j) i k -> p j (i k)", j=4
                    ),
                )
                c_raw[(blk, g)] = raw
            for g in range(NG):
                raw = wring.tile([P, 4, BLK], BF16, tag="w_raw", name="w_raw")
                nc.sync.dma_start(
                    out=raw[:],
                    in_=base_weight[512 * g : 512 * (g + 1), BLK * blk : BLK * (blk + 1)].rearrange(
                        "(p j) c -> p j c", j=4
                    ),
                )
                w_raw[(blk, g)] = raw

        def activations(blk):
            cs = slice(BLK * blk, BLK * (blk + 1))
            th = fac3.tile([P, NB, BLK], F32, tag="th", name="th")
            nc.scalar.activation(out=th[:], in_=x_sb[:, :, cs], func=ACT.Tanh)
            ut = fac3.tile([P, NB, BLK], F32, tag="ut", name="ut")
            nc.scalar.activation(out=ut[:], in_=th[:], func=ACT.Square, scale=math.sqrt(lam))
            sq = work.tile([P, NB, BLK], F32, tag="sq", name="sq")
            nc.scalar.activation(
                out=sq[:], in_=ut[:], func=ACT.Square, scale=math.sqrt(ks) / lam, bias=math.sqrt(ks) * alpha
            )
            facs[blk] = (th, ut, sq)

        def regroup(blk):
            for g in range(NG):
                view = c_raw[(blk, g)][:].rearrange("p j (i k) -> p i j k", k=6)
                t1 = stage1.tile([P, 4, BLK, 4], BF16, tag="t1", name="t1", align_bytes=64)
                t2 = stage2.tile([P, 2, BLK, 4], BF16, tag="t2", name="t2", align_bytes=64)
                copy_on((blk, g) in V123, t1[:, 0:3, :, :].rearrange("p k i j -> p i j k"), view[:, :, :, 1:4])
                copy_on(
                    (blk, g) in VW,
                    t1[:, 3, :, :].rearrange("p (c i) t -> p c t i", i=4),
                    w_raw[(blk, g)][:].rearrange("p t (c i) -> p c t i", i=4),
                )
                copy_on((blk, g) in V45, t2[:].rearrange("p k i j -> p i j k"), view[:, :, :, 4:6])
                grp[(blk, g)] = (t1, t2)

        def quantise(blk):
            for g in range(NG):
                cd = codes.tile([P, 1024], U32, tag="codes1", name="cd1", align_bytes=64)
                sc = codes.tile([P, 1024], U8, tag="scales1", name="sc1", align_bytes=64)
                nc.vector.quantize_mx(
                    out=cd[:].bitcast(E4M3X4), scales=sc[:], in_=grp[(blk, g)][0][:].rearrange("p k i j -> p (k i j)")
                )
                opnd[("Y", blk, g)] = (cd[:, 0:512], sc[:, 0:512])
                opnd[("Z", blk, g)] = (cd[:, 512:1024], sc[:, 512:1024])
            for g in range(NG):
                cd = codes.tile([P, 512], U32, tag="codes2", name="cd2", align_bytes=64)
                sc = codes.tile([P, 512], U8, tag="scales2", name="sc2", align_bytes=64)
                nc.vector.quantize_mx(
                    out=cd[:].bitcast(E4M3X4), scales=sc[:], in_=grp[(blk, g)][1][:].rearrange("p k i j -> p (k i j)")
                )
                opnd[("X", blk, g)] = (cd[:], sc[:])

        def multiply(kind, blk):
            tiles = []
            for bt in range(NB):
                bank = psum.tile([P, 512], F32, tag="bank", name="bank")
                for g in range(NG):
                    sl = slice((g * NB + bt) * P, (g * NB + bt + 1) * P)
                    cd, sc = opnd[(kind, blk, g)]
                    nc.tensor.matmul_mx(
                        out=bank[:],
                        lhsT=g_codes[:, sl].bitcast(E5M2X4),
                        lhsT_scale=g_scales[:, sl],
                        rhs=cd.bitcast(E4M3X4),
                        rhs_scale=sc,
                        start=(g == 0),
                        stop=(g == NG - 1),
                    )
                tiles.append(bank)
            banks[(kind, blk)] = tiles

        def leave_z(blk):
            th, ut, sq = facs[blk]
            a1 = work.tile([P, NB, BLK], F32, tag="a1", name="a1")
            p0 = work.tile([P, NB, BLK], F32, tag="p0", name="p0")
            for bt in range(NB):
                pz = banks[("Z", blk)][bt]
                stt(a1[:, bt, :], ut[:, bt, :], lam * r3, pz[:, 0:BLK], ALU.add, ALU.mult)
                stt(p0[:, bt, :], pz[:, BLK:512], -1.0, nf0[blk][:, bt, :], ALU.mult, ALU.mult)
            res[blk] = [a1, p0]

        def leave_x(blk):
            th, ut, sq = facs[blk]
            a2 = work.tile([P, NB, BLK], F32, tag="a2", name="a2")
            p5 = work.tile([P, NB, BLK], F32, tag="p5", name="p5")
            for bt in range(NB):
                px = banks[("X", blk)][bt]
                stt(a2[:, bt, :], ut[:, bt, :], lam * r4, px[:, 0:BLK], ALU.add, ALU.mult)
                stt(p5[:, bt, :], sq[:, bt, :], ks * beta, px[:, BLK:512], ALU.add, ALU.mult)
            res[blk].extend([a2, p5])

        def leave_y(blk):
            a1, p0, a2, p5 = res[blk]
            for bt in range(NB):
                py = banks[("Y", blk)][bt]
                stt(a1[:, bt, :], py[:, 0:BLK], 2.0 * lam / c31, a1[:, bt, :], ALU.mult, ALU.add)
                stt(a2[:, bt, :], py[:, BLK:512], lam * c2 / c41, a2[:, bt, :], ALU.mult, ALU.add)

        def join_first(blk, eng, bs):
            a1, p0, a2, p5 = res[blk]
            eng.tensor_tensor(out=a2[:, bs, :], in0=a2[:, bs, :], in1=facs[blk][0][:, bs, :], op=ALU.mult)
            eng.tensor_tensor(out=a1[:, bs, :], in0=a1[:, bs, :], in1=p5[:, bs, :], op=ALU.add)

        def join_second(blk, bs):
            a1, p0, a2, p5 = res[blk]
            stt(a1[:, bs, :], a2[:, bs, :], c41 / c31, a1[:, bs, :], ALU.mult, ALU.add)
            stt(a1[:, bs, :], facs[blk][1][:, bs, :], -lam, a1[:, bs, :], ALU.add, ALU.mult)

        def finish(blk, eng, queue, bs):
            a1, p0, a2, p5 = res[blk]
            eng.tensor_tensor(out=a2[:, bs, :], in0=p0[:, bs, :], in1=a1[:, bs, :], op=ALU.subtract)
            queue.dma_start(out=out_v[:, bs, BLK * blk : BLK * (blk + 1)], in_=a2[:, bs, :])

        def prepare(blk):
            activations(blk)
            regroup(blk)
            if blk + 2 < NBLK:
                load_block(blk + 2)

        side = nc.gpsimd if GP_OPS else nc.vector
        whole = slice(0, NB)

        load_block(0)
        tags = ("a1", "p0", "a2", "p5")
        for blk in range(NBLK):
            cs = slice(BLK * blk, BLK * (blk + 1))
            s_t[blk] = work.tile([P, NB, BLK], F32, tag=tags[blk // 2], name="s_sb")
            nc.scalar.activation(out=s_t[blk][:], in_=x_sb[:, :, cs], func=ACT.Sigmoid)
        for blk in range(NBLK):
            cs = slice(BLK * blk, BLK * (blk + 1))
            y_t[blk] = work.tile([P, NB, BLK], F32, tag=tags[2 + blk // 2], name="y_sb")
            nc.scalar.activation(out=y_t[blk][:], in_=x_sb[:, :, cs], func=ACT.Silu, scale=-1.0)
        g32 = g_sb[:].bitcast(F32).rearrange("p n (g w u) -> p n g w u", g=NG, u=2)
        g_grp32 = g_grp[:].bitcast(F32).rearrange("p (s b u) -> p s b u", s=NG * NB, u=2)
        for pr in range(NG * NB // 2):
            gt = psum.tile([P, 2, 2, P], F32, tag="bank", name="gt")
            for h in range(2):
                g, bt = divmod(2 * pr + h, NB)
                for u in range(2):
                    nc.tensor.transpose(gt[:, h, u, :], g32[:, bt, g, :, u], ident[:])
            nc.vector.tensor_copy(
                out=g_grp32[:, 2 * pr : 2 * pr + 2, :, :], in_=gt[:].rearrange("p h u b -> p h b u")
            )
        g_codes = keep.tile([P, NG * NB * P], U32, name="g_codes", align_bytes=64)
        g_scales = keep.tile([P, NG * NB * P], U8, name="g_scales", align_bytes=64)
        nc.vector.quantize_mx(out=g_codes[:].bitcast(E5M2X4), scales=g_scales[:], in_=g_grp[:])
        load_block(1)
        for blk in range(NBLK):
            nf0[blk] = keep.tile([P, NB, BLK], F32, name="nf0_%d" % blk)
            stt(nf0[blk][:], y_t[blk][:], -1.0, s_t[blk][:], ALU.add, ALU.mult)

        prepare(0)
        quantise(0)
        multiply("Z", 0)
        multiply("X", 0)

        for blk in range(NBLK):
            more = blk + 1 < NBLK
            leave_z(blk)
            multiply("Y", blk)
            leave_x(blk)
            if blk > 0:
                join_second(blk - 1, whole)
                finish(blk - 1, side, nc.sync, whole)
            leave_y(blk)
            if more:
                join_first(blk, side, whole)
                prepare(blk + 1)
                quantise(blk + 1)
                multiply("Z", blk + 1)
                multiply("X", blk + 1)
        for half in range(2):
            bs = slice(2 * half, 2 * half + 2)
            join_first(NBLK - 1, nc.vector, bs)
            join_second(NBLK - 1, bs)
            finish(NBLK - 1, nc.vector, nc.sync, bs)
